import numpy as np
import ml_dtypes

BF16 = ml_dtypes.bfloat16


def bf(x):
    return np.asarray(x, np.float32).astype(BF16)


def f32(x):
    return np.asarray(x, np.float32)


def f64(x):
    return np.asarray(x).astype(np.float64)


def striped(idx):
    return np.tile(idx.reshape(-1, 16).T, (8, 1))


C, S, B, T, N = 512, 4096, 4, 512, 2048
EPS = 1e-5


def setup_inputs():
    return {
        "words": f32(np.random.standard_normal((C, S))),
        "pos": f32(np.random.standard_normal((C, T))),
        "tok": f32(0.5 * np.random.standard_normal((C, 1))),
        "gamma": f32(1.0 + 0.1 * np.random.standard_normal((C, 1))),
        "beta": f32(0.1 * np.random.standard_normal((C, 1))),
        "offs": striped(np.random.permutation(np.tile(np.arange(S), 2))[:N]),
    }


def reference(words, pos, tok, gamma, beta, offs):
    idx = offs[:16].T.reshape(-1)
    x = f64(words)[:, idx] + np.tile(f64(pos), (1, B)) + f64(tok)
    mean = x.mean(axis=0, keepdims=True)
    var = np.square(x - mean).mean(axis=0, keepdims=True)
    return f64(gamma) * (x - mean) / np.sqrt(var + EPS) + f64(beta)

@@ -1,0 +1,101 @@
+import concourse.mybir as mybir
+from concourse.masks import make_identity
+
+F32 = mybir.dt.float32
+BF16 = mybir.dt.bfloat16
+U16 = mybir.dt.uint16
+ADD = mybir.AluOpType.add
+SUBTRACT = mybir.AluOpType.subtract
+MULT = mybir.AluOpType.mult
+FUNC = mybir.ActivationFunctionType
+
+P = 128
+C = 512
+S = 4096
+T = 512
+B = 4
+N = B * T
+KB = C // P
+EPS = 1e-5
+
+
+def tile_pclembeddings_kernel(tc, words, pos, tok, gamma, beta, offs, out):
+    nc = tc.nc
+    words_blocks = words.rearrange("(k p) s -> k p s", p=P)
+    pos_blocks = pos.rearrange("(k p) t -> k p t", p=P)
+    out_blocks = out.rearrange("(k p) n -> k p n", p=P)
+
+    with (
+        tc.tile_pool(name="held", bufs=1) as held,
+        tc.tile_pool(name="work", bufs=4) as work,
+        tc.psum_pool(name="psum_held", bufs=1) as psum_held,
+        tc.psum_pool(name="psum_var", bufs=3) as psum_var,
+    ):
+        offsets = held.tile([P, N // 16], U16, name="offsets")
+        nc.sync.dma_start(offsets[:], offs)
+
+        rows = held.tile([P, P], F32, name="rows")
+        nc.vector.memset(rows[:], 0.0)
+        for i, vector in enumerate((tok, gamma, beta)):
+            nc.scalar.dma_start(rows[i * KB : (i + 1) * KB, :], vector.rearrange("(k p) o -> k (p o)", p=P))
+
+        postok = [held.tile([P, T], F32, name=f"postok{k}") for k in range(KB)]
+        table = [held.tile([P, S], F32, name=f"table{k}") for k in range(KB)]
+        for k in range(KB):
+            nc.sync.dma_start(postok[k][:], pos_blocks[k])
+            nc.sync.dma_start(table[k][:], words_blocks[k])
+
+        identity = held.tile([P, P], F32, name="identity")
+        make_identity(nc, identity[:])
+        columns_psum = psum_held.tile([P, P], F32, name="columns_psum")
+        nc.tensor.transpose(columns_psum[:], rows[:], identity[:])
+        columns = held.tile([P, 3 * KB], F32, name="columns")
+        nc.vector.tensor_copy(columns[:], columns_psum[:, 0 : 3 * KB])
+        tok_col = [columns[:, 0 * KB + k : 0 * KB + k + 1] for k in range(KB)]
+        gamma_col = [columns[:, 1 * KB + k : 1 * KB + k + 1] for k in range(KB)]
+        beta_col = [columns[:, 2 * KB + k : 2 * KB + k + 1] for k in range(KB)]
+
+        average_f32 = held.tile([P, P], F32, name="average_f32")
+        nc.vector.memset(average_f32[:], 1.0 / C)
+        average_bf16 = held.tile([P, P], BF16, name="average_bf16")
+        nc.vector.memset(average_bf16[:], 1.0 / C)
+        eps = held.tile([P, 1], F32, name="eps")
+        nc.vector.memset(eps[:], EPS)
+
+        for k in range(KB):
+            nc.vector.tensor_scalar_add(postok[k][:], postok[k][:], tok_col[k])
+
+        x = [held.tile([P, N], F32, name=f"x{k}") for k in range(KB)]
+        mean = [psum_held.tile([P, T], F32, name=f"mean{b}") for b in range(B)]
+
+        def look_up(k, b):
+            piece = offsets[:, b * (T // 16) : (b + 1) * (T // 16)]
+            x_kb = x[k][:, b * T : (b + 1) * T]
+            nc.vector.tensor_tensor(x_kb, table[k][:].indirect(piece), postok[k][:], ADD)
+            nc.tensor.matmul(mean[b][:], average_f32[:], x_kb, start=(k == 0), stop=(k == KB - 1))
+
+        def normalise(b):
+            centred = []
+            var = psum_var.tile([P, T], F32, name="var")
+            for k in range(KB):
+                d = work.tile([P, T], F32, name="d", bufs=3 * KB)
+                nc.vector.tensor_tensor(d[:], x[k][:, b * T : (b + 1) * T], mean[b][:], SUBTRACT)
+                square = work.tile([P, T], BF16, name="square")
+                nc.scalar.activation(square[:], d[:], FUNC.Square)
+                nc.tensor.matmul(var[:], average_bf16[:], square[:], start=(k == 0), stop=(k == KB - 1))
+                centred.append(d)
+            rstd = work.tile([P, T], F32, name="rstd", bufs=2)
+            nc.scalar.activation(rstd[:], var[:], FUNC.Abs_reciprocal_sqrt, bias=eps[:])
+            for k in range(KB):
+                z = work.tile([P, T], F32, name="z")
+                nc.vector.tensor_tensor(z[:], centred[k][:], rstd[:], MULT)
+                y = work.tile([P, T], F32, name="y")
+                nc.scalar.activation(y[:], z[:], FUNC.Identity, bias=beta_col[k], scale=gamma_col[k])
+                nc.sync.dma_start(out_blocks[k][:, b * T : (b + 1) * T], y[:])
+
+        for k in range(KB - 1):
+            for b in range(B):
+                look_up(k, b)
+        for b in range(B):
+            look_up(KB - 1, b)
+            normalise(b)

@@ -31,13 +31,13 @@ def tile_pclembeddings_kernel(tc, words, pos, tok, gamma, beta, offs, out):
         tc.psum_pool(name="psum_held", bufs=1) as psum_held,
         tc.psum_pool(name="psum_var", bufs=3) as psum_var,
     ):
+        rows = held.tile([P, P], F32, name="rows")
+        nc.gpsimd.memset(rows[:], 0.0)
+        for i, vector in enumerate((tok, gamma, beta)):
+            nc.sync.dma_start(rows[i * KB : (i + 1) * KB, :], vector.rearrange("(k p) o -> k (p o)", p=P))
+
         offsets = held.tile([P, N // 16], U16, name="offsets")
         nc.sync.dma_start(offsets[:], offs)
-
-        rows = held.tile([P, P], F32, name="rows")
-        nc.vector.memset(rows[:], 0.0)
-        for i, vector in enumerate((tok, gamma, beta)):
-            nc.scalar.dma_start(rows[i * KB : (i + 1) * KB, :], vector.rearrange("(k p) o -> k (p o)", p=P))
 
         postok = [held.tile([P, T], F32, name=f"postok{k}") for k in range(KB)]
         table = [held.tile([P, S], F32, name=f"table{k}") for k in range(KB)]
@@ -88,9 +88,13 @@ def tile_pclembeddings_kernel(tc, words, pos, tok, gamma, beta, offs, out):
             nc.scalar.activation(rstd[:], var[:], FUNC.Abs_reciprocal_sqrt, bias=eps[:])
             for k in range(KB):
                 z = work.tile([P, T], F32, name="z")
-                nc.vector.tensor_tensor(z[:], centred[k][:], rstd[:], MULT)
                 y = work.tile([P, T], F32, name="y")
-                nc.scalar.activation(y[:], z[:], FUNC.Identity, bias=beta_col[k], scale=gamma_col[k])
+                if k < KB // 2:
+                    nc.vector.tensor_tensor(z[:], centred[k][:], rstd[:], MULT)
+                    nc.scalar.activation(y[:], z[:], FUNC.Identity, bias=beta_col[k], scale=gamma_col[k])
+                else:
+                    nc.gpsimd.tensor_tensor(z[:], centred[k][:], rstd[:], MULT)
+                    nc.gpsimd.tensor_scalar(y[:], z[:], gamma_col[k], beta_col[k], MULT, ADD)
                 nc.sync.dma_start(out_blocks[k][:, b * T : (b + 1) * T], y[:])
 
         for k in range(KB - 1):

@@ -89,12 +89,8 @@ def tile_pclembeddings_kernel(tc, words, pos, tok, gamma, beta, offs, out):
             for k in range(KB):
                 z = work.tile([P, T], F32, name="z")
                 y = work.tile([P, T], F32, name="y")
-                if k < KB // 2:
-                    nc.vector.tensor_tensor(z[:], centred[k][:], rstd[:], MULT)
-                    nc.scalar.activation(y[:], z[:], FUNC.Identity, bias=beta_col[k], scale=gamma_col[k])
-                else:
-                    nc.gpsimd.tensor_tensor(z[:], centred[k][:], rstd[:], MULT)
-                    nc.gpsimd.tensor_scalar(y[:], z[:], gamma_col[k], beta_col[k], MULT, ADD)
+                nc.vector.tensor_tensor(z[:], centred[k][:], rstd[:], MULT)
+                nc.scalar.activation(y[:], z[:], FUNC.Identity, bias=beta_col[k], scale=gamma_col[k])
                 nc.sync.dma_start(out_blocks[k][:, b * T : (b + 1) * T], y[:])
 
         for k in range(KB - 1):

@@ -67,6 +67,8 @@ def tile_pclembeddings_kernel(tc, words, pos, tok, gamma, beta, offs, out):
 
         x = [held.tile([P, N], F32, name=f"x{k}") for k in range(KB)]
         mean = [psum_held.tile([P, T], F32, name=f"mean{b}") for b in range(B)]
+        d = [held.tile([P, N], F32, name=f"d{k}") for k in range(KB)]
+        rstd = [held.tile([P, T], F32, name=f"rstd{b}") for b in range(B)]
 
         def look_up(k, b):
             piece = offsets[:, b * (T // 16) : (b + 1) * (T // 16)]
@@ -74,28 +76,32 @@ def tile_pclembeddings_kernel(tc, words, pos, tok, gamma, beta, offs, out):
             nc.vector.tensor_tensor(x_kb, table[k][:].indirect(piece), postok[k][:], ADD)
             nc.tensor.matmul(mean[b][:], average_f32[:], x_kb, start=(k == 0), stop=(k == KB - 1))
 
-        def normalise(b):
-            centred = []
+        def centre(b):
             var = psum_var.tile([P, T], F32, name="var")
             for k in range(KB):
-                d = work.tile([P, T], F32, name="d", bufs=3 * KB)
-                nc.vector.tensor_tensor(d[:], x[k][:, b * T : (b + 1) * T], mean[b][:], SUBTRACT)
+                d_kb = d[k][:, b * T : (b + 1) * T]
+                nc.vector.tensor_tensor(d_kb, x[k][:, b * T : (b + 1) * T], mean[b][:], SUBTRACT)
                 square = work.tile([P, T], BF16, name="square")
-                nc.scalar.activation(square[:], d[:], FUNC.Square)
+                nc.scalar.activation(square[:], d_kb, FUNC.Square)
                 nc.tensor.matmul(var[:], average_bf16[:], square[:], start=(k == 0), stop=(k == KB - 1))
-                centred.append(d)
-            rstd = work.tile([P, T], F32, name="rstd", bufs=2)
-            nc.scalar.activation(rstd[:], var[:], FUNC.Abs_reciprocal_sqrt, bias=eps[:])
+            nc.scalar.activation(rstd[b][:], var[:], FUNC.Abs_reciprocal_sqrt, bias=eps[:])
+
+        def scale(b):
             for k in range(KB):
-                z = work.tile([P, T], F32, name="z")
-                y = work.tile([P, T], F32, name="y")
-                nc.vector.tensor_tensor(z[:], centred[k][:], rstd[:], MULT)
-                nc.scalar.activation(y[:], z[:], FUNC.Identity, bias=beta_col[k], scale=gamma_col[k])
+                z = work.tile([P, T], F32, name="z", bufs=6)
+                nc.vector.tensor_tensor(z[:], d[k][:, b * T : (b + 1) * T], rstd[b][:], MULT)
+                y = work.tile([P, T], F32, name="y", bufs=8)
+                if k < KB - 1:
+                    nc.scalar.activation(y[:], z[:], FUNC.Identity, bias=beta_col[k], scale=gamma_col[k])
+                else:
+                    nc.vector.tensor_scalar(y[:], z[:], gamma_col[k], beta_col[k], MULT, ADD)
                 nc.sync.dma_start(out_blocks[k][:, b * T : (b + 1) * T], y[:])
 
-        for k in range(KB - 1):
+        for k in range(KB):
             for b in range(B):
                 look_up(k, b)
-        for b in range(B):
-            look_up(KB - 1, b)
-            normalise(b)
+        centre(0)
+        for b in range(1, B):
+            centre(b)
+            scale(b - 1)
+        scale(B - 1)

@@ -25,12 +25,7 @@ def tile_pclembeddings_kernel(tc, words, pos, tok, gamma, beta, offs, out):
     pos_blocks = pos.rearrange("(k p) t -> k p t", p=P)
     out_blocks = out.rearrange("(k p) n -> k p n", p=P)
 
-    with (
-        tc.tile_pool(name="held", bufs=1) as held,
-        tc.tile_pool(name="work", bufs=4) as work,
-        tc.psum_pool(name="psum_held", bufs=1) as psum_held,
-        tc.psum_pool(name="psum_var", bufs=3) as psum_var,
-    ):
+    with tc.tile_pool(name="held", bufs=1) as held, tc.tile_pool(name="work", bufs=4) as work:
         rows = held.tile([P, P], F32, name="rows")
         nc.gpsimd.memset(rows[:], 0.0)
         for i, vector in enumerate((tok, gamma, beta)):
@@ -47,10 +42,11 @@ def tile_pclembeddings_kernel(tc, words, pos, tok, gamma, beta, offs, out):
 
         identity = held.tile([P, P], F32, name="identity")
         make_identity(nc, identity[:])
-        columns_psum = psum_held.tile([P, P], F32, name="columns_psum")
-        nc.tensor.transpose(columns_psum[:], rows[:], identity[:])
         columns = held.tile([P, 3 * KB], F32, name="columns")
-        nc.vector.tensor_copy(columns[:], columns_psum[:, 0 : 3 * KB])
+        with tc.psum_pool(name="psum_setup", bufs=1) as psum_setup:
+            columns_psum = psum_setup.tile([P, P], F32, name="columns_psum")
+            nc.tensor.transpose(columns_psum[:], rows[:], identity[:])
+            nc.vector.tensor_copy(columns[:], columns_psum[:, 0 : 3 * KB])
         tok_col = [columns[:, 0 * KB + k : 0 * KB + k + 1] for k in range(KB)]
         gamma_col = [columns[:, 1 * KB + k : 1 * KB + k + 1] for k in range(KB)]
         beta_col = [columns[:, 2 * KB + k : 2 * KB + k + 1] for k in range(KB)]
@@ -63,45 +59,50 @@ def tile_pclembeddings_kernel(tc, words, pos, tok, gamma, beta, offs, out):
         nc.vector.memset(eps[:], EPS)
 
         for k in range(KB):
-            nc.vector.tensor_scalar_add(postok[k][:], postok[k][:], tok_col[k])
+            nc.scalar.activation(postok[k][:], postok[k][:], FUNC.Identity, bias=tok_col[k])
 
         x = [held.tile([P, N], F32, name=f"x{k}") for k in range(KB)]
-        mean = [psum_held.tile([P, T], F32, name=f"mean{b}") for b in range(B)]
         d = [held.tile([P, N], F32, name=f"d{k}") for k in range(KB)]
         rstd = [held.tile([P, T], F32, name=f"rstd{b}") for b in range(B)]
 
-        def look_up(k, b):
-            piece = offsets[:, b * (T // 16) : (b + 1) * (T // 16)]
-            x_kb = x[k][:, b * T : (b + 1) * T]
-            nc.vector.tensor_tensor(x_kb, table[k][:].indirect(piece), postok[k][:], ADD)
-            nc.tensor.matmul(mean[b][:], average_f32[:], x_kb, start=(k == 0), stop=(k == KB - 1))
+        with tc.psum_pool(name="psum_held", bufs=1) as psum_held, tc.psum_pool(name="psum_work", bufs=3) as psum_work:
+            mean = [psum_held.tile([P, T], F32, name=f"mean{b}") for b in range(B)]
 
-        def centre(b):
-            var = psum_var.tile([P, T], F32, name="var")
-            for k in range(KB):
-                d_kb = d[k][:, b * T : (b + 1) * T]
-                nc.vector.tensor_tensor(d_kb, x[k][:, b * T : (b + 1) * T], mean[b][:], SUBTRACT)
-                square = work.tile([P, T], BF16, name="square")
-                nc.scalar.activation(square[:], d_kb, FUNC.Square)
-                nc.tensor.matmul(var[:], average_bf16[:], square[:], start=(k == 0), stop=(k == KB - 1))
-            nc.scalar.activation(rstd[b][:], var[:], FUNC.Abs_reciprocal_sqrt, bias=eps[:])
+            def look_up(k, b):
+                piece = offsets[:, b * (T // 16) : (b + 1) * (T // 16)]
+                x_kb = x[k][:, b * T : (b + 1) * T]
+                nc.vector.tensor_tensor(x_kb, table[k][:].indirect(piece), postok[k][:], ADD)
+                nc.tensor.matmul(mean[b][:], average_f32[:], x_kb, start=(k == 0), stop=(k == KB - 1))
 
-        def scale(b):
-            for k in range(KB):
-                z = work.tile([P, T], F32, name="z", bufs=6)
-                nc.vector.tensor_tensor(z[:], d[k][:, b * T : (b + 1) * T], rstd[b][:], MULT)
-                y = work.tile([P, T], F32, name="y", bufs=8)
-                if k < KB - 1:
-                    nc.scalar.activation(y[:], z[:], FUNC.Identity, bias=beta_col[k], scale=gamma_col[k])
-                else:
-                    nc.vector.tensor_scalar(y[:], z[:], gamma_col[k], beta_col[k], MULT, ADD)
-                nc.sync.dma_start(out_blocks[k][:, b * T : (b + 1) * T], y[:])
+            def centre(b):
+                var = psum_work.tile([P, T], F32, name="var")
+                for k in range(KB):
+                    d_kb = d[k][:, b * T : (b + 1) * T]
+                    nc.vector.tensor_tensor(d_kb, x[k][:, b * T : (b + 1) * T], mean[b][:], SUBTRACT)
+                    square = work.tile([P, T], BF16, name="square")
+                    nc.scalar.activation(square[:], d_kb, FUNC.Square)
+                    nc.tensor.matmul(var[:], average_bf16[:], square[:], start=(k == 0), stop=(k == KB - 1))
+                nc.scalar.activation(rstd[b][:], var[:], FUNC.Abs_reciprocal_sqrt, bias=eps[:])
 
-        for k in range(KB):
-            for b in range(B):
-                look_up(k, b)
-        centre(0)
-        for b in range(1, B):
-            centre(b)
-            scale(b - 1)
-        scale(B - 1)
+            def scale(b):
+                for k in range(KB):
+                    d_kb = d[k][:, b * T : (b + 1) * T]
+                    z = work.tile([P, T], F32, name="z", bufs=6)
+                    y = work.tile([P, T], F32, name="y", bufs=8)
+                    nc.vector.tensor_tensor(z[:], d_kb, rstd[b][:], MULT)
+                    if k < KB - 1:
+                        nc.scalar.activation(y[:], z[:], FUNC.Identity, bias=beta_col[k], scale=gamma_col[k])
+                    else:
+                        nc.vector.tensor_scalar(y[:], z[:], gamma_col[k], beta_col[k], MULT, ADD)
+                    nc.sync.dma_start(out_blocks[k][:, b * T : (b + 1) * T], y[:])
+
+            for k in range(KB - 1):
+                for b in range(B):
+                    look_up(k, b)
+            for b in range(B + 2):
+                if b < B:
+                    look_up(KB - 1, b)
+                if 1 <= b <= B:
+                    centre(b - 1)
+                if b >= 2:
+                    scale(b - 2)

@@ -61,7 +61,11 @@ def tile_pclembeddings_kernel(tc, words, pos, tok, gamma, beta, offs, out):
         for k in range(KB):
             nc.scalar.activation(postok[k][:], postok[k][:], FUNC.Identity, bias=tok_col[k])
 
-        x = [held.tile([P, N], F32, name=f"x{k}") for k in range(KB)]
+        x = [held.tile([P, N], F32, name=f"x{k}") for k in range(KB - 1)]
+        x_piece = {}
+        for k in range(KB - 1):
+            for b in range(B):
+                x_piece[k, b] = x[k][:, b * T : (b + 1) * T]
         d = [held.tile([P, N], F32, name=f"d{k}") for k in range(KB)]
         rstd = [held.tile([P, T], F32, name=f"rstd{b}") for b in range(B)]
 
@@ -70,7 +74,10 @@ def tile_pclembeddings_kernel(tc, words, pos, tok, gamma, beta, offs, out):
 
             def look_up(k, b):
                 piece = offsets[:, b * (T // 16) : (b + 1) * (T // 16)]
-                x_kb = x[k][:, b * T : (b + 1) * T]
+                if k == KB - 1:
+                    x_last = work.tile([P, T], F32, name="x_last", bufs=3)
+                    x_piece[k, b] = x_last[:]
+                x_kb = x_piece[k, b]
                 nc.vector.tensor_tensor(x_kb, table[k][:].indirect(piece), postok[k][:], ADD)
                 nc.tensor.matmul(mean[b][:], average_f32[:], x_kb, start=(k == 0), stop=(k == KB - 1))
 
@@ -78,7 +85,7 @@ def tile_pclembeddings_kernel(tc, words, pos, tok, gamma, beta, offs, out):
                 var = psum_work.tile([P, T], F32, name="var")
                 for k in range(KB):
                     d_kb = d[k][:, b * T : (b + 1) * T]
-                    nc.vector.tensor_tensor(d_kb, x[k][:, b * T : (b + 1) * T], mean[b][:], SUBTRACT)
+                    nc.vector.tensor_tensor(d_kb, x_piece[k, b], mean[b][:], SUBTRACT)
                     square = work.tile([P, T], BF16, name="square")
                     nc.scalar.activation(square[:], d_kb, FUNC.Square)
                     nc.tensor.matmul(var[:], average_bf16[:], square[:], start=(k == 0), stop=(k == KB - 1))
@@ -99,10 +106,10 @@ def tile_pclembeddings_kernel(tc, words, pos, tok, gamma, beta, offs, out):
             for k in range(KB - 1):
                 for b in range(B):
                     look_up(k, b)
-            for b in range(B + 2):
+            for b in range(B + 1):
                 if b < B:
                     look_up(KB - 1, b)
-                if 1 <= b <= B:
+                if b >= 1:
                     centre(b - 1)
-                if b >= 2:
-                    scale(b - 2)
+            for b in range(B):
+                scale(b)

@@ -97,7 +97,7 @@ def tile_pclembeddings_kernel(tc, words, pos, tok, gamma, beta, offs, out):
                     z = work.tile([P, T], F32, name="z", bufs=6)
                     y = work.tile([P, T], F32, name="y", bufs=8)
                     nc.vector.tensor_tensor(z[:], d_kb, rstd[b][:], MULT)
-                    if k < KB - 1:
+                    if b > 0:
                         nc.scalar.activation(y[:], z[:], FUNC.Identity, bias=beta_col[k], scale=gamma_col[k])
                     else:
                         nc.vector.tensor_scalar(y[:], z[:], gamma_col[k], beta_col[k], MULT, ADD)

@@ -17,6 +17,8 @@ B = 4
 N = B * T
 KB = C // P
 EPS = 1e-5
+PIECES = [(0, T // 2), (T // 2, T // 2)] + [(b * T, T) for b in range(1, B)]
+FIRST_SEQUENCE = 2
 
 
 def tile_pclembeddings_kernel(tc, words, pos, tok, gamma, beta, offs, out):
@@ -64,52 +66,54 @@ def tile_pclembeddings_kernel(tc, words, pos, tok, gamma, beta, offs, out):
         x = [held.tile([P, N], F32, name=f"x{k}") for k in range(KB - 1)]
         x_piece = {}
         for k in range(KB - 1):
-            for b in range(B):
-                x_piece[k, b] = x[k][:, b * T : (b + 1) * T]
+            for i, (first, width) in enumerate(PIECES):
+                x_piece[k, i] = x[k][:, first : first + width]
         d = [held.tile([P, N], F32, name=f"d{k}") for k in range(KB)]
-        rstd = [held.tile([P, T], F32, name=f"rstd{b}") for b in range(B)]
+        rstd = held.tile([P, N], F32, name="rstd")
 
         with tc.psum_pool(name="psum_held", bufs=1) as psum_held, tc.psum_pool(name="psum_work", bufs=3) as psum_work:
-            mean = [psum_held.tile([P, T], F32, name=f"mean{b}") for b in range(B)]
+            mean = [psum_held.tile([P, T], F32, name=f"mean{i}")[:, 0:width] for i, (first, width) in enumerate(PIECES)]
 
-            def look_up(k, b):
-                piece = offsets[:, b * (T // 16) : (b + 1) * (T // 16)]
+            def look_up(k, i):
+                first, width = PIECES[i]
+                piece = offsets[:, first // 16 : (first + width) // 16]
                 if k == KB - 1:
                     x_last = work.tile([P, T], F32, name="x_last", bufs=3)
-                    x_piece[k, b] = x_last[:]
-                x_kb = x_piece[k, b]
-                nc.vector.tensor_tensor(x_kb, table[k][:].indirect(piece), postok[k][:], ADD)
-                nc.tensor.matmul(mean[b][:], average_f32[:], x_kb, start=(k == 0), stop=(k == KB - 1))
+                    x_piece[k, i] = x_last[:, 0:width]
+                x_ki = x_piece[k, i]
+                nc.vector.tensor_tensor(x_ki, table[k][:].indirect(piece), postok[k][:, first % T : first % T + width], ADD)
+                nc.tensor.matmul(mean[i], average_f32[:], x_ki, start=(k == 0), stop=(k == KB - 1))
 
-            def centre(b):
+            def centre(i):
+                first, width = PIECES[i]
                 var = psum_work.tile([P, T], F32, name="var")
                 for k in range(KB):
-                    d_kb = d[k][:, b * T : (b + 1) * T]
-                    nc.vector.tensor_tensor(d_kb, x_piece[k, b], mean[b][:], SUBTRACT)
+                    d_ki = d[k][:, first : first + width]
+                    nc.vector.tensor_tensor(d_ki, x_piece[k, i], mean[i], SUBTRACT)
                     square = work.tile([P, T], BF16, name="square")
-                    nc.scalar.activation(square[:], d_kb, FUNC.Square)
-                    nc.tensor.matmul(var[:], average_bf16[:], square[:], start=(k == 0), stop=(k == KB - 1))
-                nc.scalar.activation(rstd[b][:], var[:], FUNC.Abs_reciprocal_sqrt, bias=eps[:])
+                    nc.scalar.activation(square[:, 0:width], d_ki, FUNC.Square)
+                    nc.tensor.matmul(var[:, 0:width], average_bf16[:], square[:, 0:width], start=(k == 0), stop=(k == KB - 1))
+                nc.scalar.activation(rstd[:, first : first + width], var[:, 0:width], FUNC.Abs_reciprocal_sqrt, bias=eps[:])
 
-            def scale(b):
+            def scale(i):
+                first, width = PIECES[i]
                 for k in range(KB):
-                    d_kb = d[k][:, b * T : (b + 1) * T]
                     z = work.tile([P, T], F32, name="z", bufs=6)
                     y = work.tile([P, T], F32, name="y", bufs=8)
-                    nc.vector.tensor_tensor(z[:], d_kb, rstd[b][:], MULT)
-                    if b > 0:
-                        nc.scalar.activation(y[:], z[:], FUNC.Identity, bias=beta_col[k], scale=gamma_col[k])
+                    nc.vector.tensor_tensor(z[:, 0:width], d[k][:, first : first + width], rstd[:, first : first + width], MULT)
+                    if i >= FIRST_SEQUENCE:
+                        nc.scalar.activation(y[:, 0:width], z[:, 0:width], FUNC.Identity, bias=beta_col[k], scale=gamma_col[k])
                     else:
-                        nc.vector.tensor_scalar(y[:], z[:], gamma_col[k], beta_col[k], MULT, ADD)
-                    nc.sync.dma_start(out_blocks[k][:, b * T : (b + 1) * T], y[:])
+                        nc.vector.tensor_scalar(y[:, 0:width], z[:, 0:width], gamma_col[k], beta_col[k], MULT, ADD)
+                    nc.sync.dma_start(out_blocks[k][:, first : first + width], y[:, 0:width])
 
             for k in range(KB - 1):
-                for b in range(B):
-                    look_up(k, b)
-            for b in range(B + 1):
-                if b < B:
-                    look_up(KB - 1, b)
-                if b >= 1:
-                    centre(b - 1)
-            for b in range(B):
-                scale(b)
+                for i in range(len(PIECES)):
+                    look_up(k, i)
+            for i in range(len(PIECES) + 1):
+                if i < len(PIECES):
+                    look_up(KB - 1, i)
+                if i >= 1:
+                    centre(i - 1)
+            for i in range(len(PIECES)):
+                scale(i)

@@ -18,7 +18,7 @@ N = B * T
 KB = C // P
 EPS = 1e-5
 PIECES = [(0, T // 2), (T // 2, T // 2)] + [(b * T, T) for b in range(1, B)]
-FIRST_SEQUENCE = 2
+VECTOR_FINISHES = 1
 
 
 def tile_pclembeddings_kernel(tc, words, pos, tok, gamma, beta, offs, out):
@@ -28,17 +28,25 @@ def tile_pclembeddings_kernel(tc, words, pos, tok, gamma, beta, offs, out):
     out_blocks = out.rearrange("(k p) n -> k p n", p=P)
 
     with tc.tile_pool(name="held", bufs=1) as held, tc.tile_pool(name="work", bufs=4) as work:
-        rows = held.tile([P, P], F32, name="rows")
-        nc.gpsimd.memset(rows[:], 0.0)
-        for i, vector in enumerate((tok, gamma, beta)):
-            nc.sync.dma_start(rows[i * KB : (i + 1) * KB, :], vector.rearrange("(k p) o -> k (p o)", p=P))
+        eps = held.tile([P, 1], F32, name="eps")
+        nc.vector.memset(eps[:], EPS)
+        table_warm_up = held.tile([P, 1], F32, name="table_warm_up")
+        nc.scalar.activation(table_warm_up[:], eps[:], FUNC.Abs_reciprocal_sqrt)
 
         offsets = held.tile([P, N // 16], U16, name="offsets")
         nc.sync.dma_start(offsets[:], offs)
 
         postok = [held.tile([P, T], F32, name=f"postok{k}") for k in range(KB)]
         table = [held.tile([P, S], F32, name=f"table{k}") for k in range(KB)]
-        for k in range(KB):
+        nc.sync.dma_start(postok[0][:], pos_blocks[0])
+
+        rows = held.tile([P, P], F32, name="rows")
+        nc.gpsimd.memset(rows[:], 0.0)
+        for i, vector in enumerate((tok, gamma, beta)):
+            nc.sync.dma_start(rows[i * KB : (i + 1) * KB, :], vector.rearrange("(k p) o -> k (p o)", p=P))
+
+        nc.sync.dma_start(table[0][:], words_blocks[0])
+        for k in range(1, KB):
             nc.sync.dma_start(postok[k][:], pos_blocks[k])
             nc.sync.dma_start(table[k][:], words_blocks[k])
 
@@ -57,8 +65,6 @@ def tile_pclembeddings_kernel(tc, words, pos, tok, gamma, beta, offs, out):
         nc.vector.memset(average_f32[:], 1.0 / C)
         average_bf16 = held.tile([P, P], BF16, name="average_bf16")
         nc.vector.memset(average_bf16[:], 1.0 / C)
-        eps = held.tile([P, 1], F32, name="eps")
-        nc.vector.memset(eps[:], EPS)
 
         for k in range(KB):
             nc.scalar.activation(postok[k][:], postok[k][:], FUNC.Identity, bias=tok_col[k])
@@ -101,7 +107,7 @@ def tile_pclembeddings_kernel(tc, words, pos, tok, gamma, beta, offs, out):
                     z = work.tile([P, T], F32, name="z", bufs=6)
                     y = work.tile([P, T], F32, name="y", bufs=8)
                     nc.vector.tensor_tensor(z[:, 0:width], d[k][:, first : first + width], rstd[:, first : first + width], MULT)
-                    if i >= FIRST_SEQUENCE:
+                    if i >= VECTOR_FINISHES:
                         nc.scalar.activation(y[:, 0:width], z[:, 0:width], FUNC.Identity, bias=beta_col[k], scale=gamma_col[k])
                     else:
                         nc.vector.tensor_scalar(y[:, 0:width], z[:, 0:width], gamma_col[k], beta_col[k], MULT, ADD)

@@ -2,7 +2,6 @@ import concourse.mybir as mybir
 from concourse.masks import make_identity
 
 F32 = mybir.dt.float32
-BF16 = mybir.dt.bfloat16
 U16 = mybir.dt.uint16
 ADD = mybir.AluOpType.add
 SUBTRACT = mybir.AluOpType.subtract
@@ -16,9 +15,10 @@ T = 512
 B = 4
 N = B * T
 KB = C // P
+G = T // P
 EPS = 1e-5
-PIECES = [(0, T // 2), (T // 2, T // 2)] + [(b * T, T) for b in range(1, B)]
-VECTOR_FINISHES = 1
+BN_STATS = 6
+BN_AGGR = 2
 
 
 def tile_pclembeddings_kernel(tc, words, pos, tok, gamma, beta, offs, out):
@@ -61,65 +61,48 @@ def tile_pclembeddings_kernel(tc, words, pos, tok, gamma, beta, offs, out):
         gamma_col = [columns[:, 1 * KB + k : 1 * KB + k + 1] for k in range(KB)]
         beta_col = [columns[:, 2 * KB + k : 2 * KB + k + 1] for k in range(KB)]
 
-        average_f32 = held.tile([P, P], F32, name="average_f32")
-        nc.vector.memset(average_f32[:], 1.0 / C)
-        average_bf16 = held.tile([P, P], BF16, name="average_bf16")
-        nc.vector.memset(average_bf16[:], 1.0 / C)
-
         for k in range(KB):
             nc.scalar.activation(postok[k][:], postok[k][:], FUNC.Identity, bias=tok_col[k])
 
-        x = [held.tile([P, N], F32, name=f"x{k}") for k in range(KB - 1)]
-        x_piece = {}
-        for k in range(KB - 1):
-            for i, (first, width) in enumerate(PIECES):
-                x_piece[k, i] = x[k][:, first : first + width]
-        d = [held.tile([P, N], F32, name=f"d{k}") for k in range(KB)]
-        rstd = held.tile([P, N], F32, name="rstd")
+        x_flipped = [held.tile([P, G * C], F32, name=f"x_flipped{b}") for b in range(B)]
 
-        with tc.psum_pool(name="psum_held", bufs=1) as psum_held, tc.psum_pool(name="psum_work", bufs=3) as psum_work:
-            mean = [psum_held.tile([P, T], F32, name=f"mean{i}")[:, 0:width] for i, (first, width) in enumerate(PIECES)]
+        with tc.psum_pool(name="psum_there", bufs=3) as psum_there, tc.psum_pool(name="psum_back", bufs=5) as psum_back:
 
-            def look_up(k, i):
-                first, width = PIECES[i]
-                piece = offsets[:, first // 16 : (first + width) // 16]
-                if k == KB - 1:
-                    x_last = work.tile([P, T], F32, name="x_last", bufs=3)
-                    x_piece[k, i] = x_last[:, 0:width]
-                x_ki = x_piece[k, i]
-                nc.vector.tensor_tensor(x_ki, table[k][:].indirect(piece), postok[k][:, first % T : first % T + width], ADD)
-                nc.tensor.matmul(mean[i], average_f32[:], x_ki, start=(k == 0), stop=(k == KB - 1))
+            def look_up(k, b):
+                x = work.tile([P, T], F32, name="x")
+                nc.vector.tensor_tensor(x[:], table[k][:].indirect(offsets[:, b * T // 16 : (b + 1) * T // 16]), postok[k][:], ADD)
+                there = psum_there.tile([P, G * P], F32, name="there")
+                for g in range(G):
+                    nc.tensor.transpose(there[:, g * P : (g + 1) * P], x[:, g * P : (g + 1) * P], identity[:])
+                by_group = x_flipped[b][:].rearrange("t (g c) -> t g c", g=G)
+                nc.scalar.activation(by_group[:, :, k * P : (k + 1) * P], there[:].rearrange("t (g c) -> t g c", g=G), FUNC.Identity)
 
-            def centre(i):
-                first, width = PIECES[i]
-                var = psum_work.tile([P, T], F32, name="var")
+            def normalise(b):
+                stats = work.tile([P, G * BN_STATS], F32, name="stats")
+                mean_var = work.tile([P, G * BN_AGGR], F32, name="mean_var")
+                for g in range(G):
+                    nc.vector.bn_stats(stats[:, g * BN_STATS : (g + 1) * BN_STATS], x_flipped[b][:, g * C : (g + 1) * C])
+                    nc.vector.bn_aggr(mean_var[:, g * BN_AGGR : (g + 1) * BN_AGGR], stats[:, g * BN_STATS : (g + 1) * BN_STATS])
+                rstd = work.tile([P, G], F32, name="rstd")
+                nc.scalar.activation(rstd[:], mean_var[:, 1 : G * BN_AGGR : BN_AGGR], FUNC.Abs_reciprocal_sqrt, bias=eps[:])
+
+                back = [psum_back.tile([P, T], F32, name="back") for k in range(KB)]
+                for g in range(G):
+                    z_flipped = work.tile([P, C], F32, name="z_flipped")
+                    mean = mean_var[:, g * BN_AGGR : g * BN_AGGR + 1]
+                    nc.vector.tensor_scalar(z_flipped[:], x_flipped[b][:, g * C : (g + 1) * C], mean, rstd[:, g : g + 1], SUBTRACT, MULT)
+                    for k in range(KB):
+                        nc.tensor.transpose(back[k][:, g * P : (g + 1) * P], z_flipped[:, k * P : (k + 1) * P], identity[:])
                 for k in range(KB):
-                    d_ki = d[k][:, first : first + width]
-                    nc.vector.tensor_tensor(d_ki, x_piece[k, i], mean[i], SUBTRACT)
-                    square = work.tile([P, T], BF16, name="square")
-                    nc.scalar.activation(square[:, 0:width], d_ki, FUNC.Square)
-                    nc.tensor.matmul(var[:, 0:width], average_bf16[:], square[:, 0:width], start=(k == 0), stop=(k == KB - 1))
-                nc.scalar.activation(rstd[:, first : first + width], var[:, 0:width], FUNC.Abs_reciprocal_sqrt, bias=eps[:])
-
-            def scale(i):
-                first, width = PIECES[i]
-                for k in range(KB):
-                    z = work.tile([P, T], F32, name="z", bufs=6)
                     y = work.tile([P, T], F32, name="y", bufs=8)
-                    nc.vector.tensor_tensor(z[:, 0:width], d[k][:, first : first + width], rstd[:, first : first + width], MULT)
-                    if i >= VECTOR_FINISHES:
-                        nc.scalar.activation(y[:, 0:width], z[:, 0:width], FUNC.Identity, bias=beta_col[k], scale=gamma_col[k])
-                    else:
-                        nc.vector.tensor_scalar(y[:, 0:width], z[:, 0:width], gamma_col[k], beta_col[k], MULT, ADD)
-                    nc.sync.dma_start(out_blocks[k][:, first : first + width], y[:, 0:width])
+                    nc.scalar.activation(y[:], back[k][:], FUNC.Identity, bias=beta_col[k], scale=gamma_col[k])
+                    nc.sync.dma_start(out_blocks[k][:, b * T : (b + 1) * T], y[:])
 
             for k in range(KB - 1):
-                for i in range(len(PIECES)):
-                    look_up(k, i)
-            for i in range(len(PIECES) + 1):
-                if i < len(PIECES):
-                    look_up(KB - 1, i)
-                if i >= 1:
-                    centre(i - 1)
-            for i in range(len(PIECES)):
-                scale(i)
+                for b in range(B):
+                    look_up(k, b)
+            for b in range(B + 1):
+                if b < B:
+                    look_up(KB - 1, b)
+                if b >= 1:
+                    normalise(b - 1)

@@ -17,6 +17,7 @@ N = B * T
 KB = C // P
 G = T // P
 EPS = 1e-5
+SCALAR_NORMALISES = 1
 BN_STATS = 6
 BN_AGGR = 2
 
@@ -83,14 +84,25 @@ def tile_pclembeddings_kernel(tc, words, pos, tok, gamma, beta, offs, out):
                 for g in range(G):
                     nc.vector.bn_stats(stats[:, g * BN_STATS : (g + 1) * BN_STATS], x_flipped[b][:, g * C : (g + 1) * C])
                     nc.vector.bn_aggr(mean_var[:, g * BN_AGGR : (g + 1) * BN_AGGR], stats[:, g * BN_STATS : (g + 1) * BN_STATS])
+                if b < SCALAR_NORMALISES:
+                    minus_mean = work.tile([P, G], F32, name="minus_mean")
+                    nc.vector.tensor_scalar_mul(minus_mean[:], mean_var[:, 0 : G * BN_AGGR : BN_AGGR], -1.0)
                 rstd = work.tile([P, G], F32, name="rstd")
                 nc.scalar.activation(rstd[:], mean_var[:, 1 : G * BN_AGGR : BN_AGGR], FUNC.Abs_reciprocal_sqrt, bias=eps[:])
+                if b < SCALAR_NORMALISES:
+                    shift = work.tile([P, G], F32, name="shift")
+                    for g in range(G):
+                        nc.scalar.activation(shift[:, g : g + 1], minus_mean[:, g : g + 1], FUNC.Identity, scale=rstd[:, g : g + 1])
 
                 back = [psum_back.tile([P, T], F32, name="back") for k in range(KB)]
                 for g in range(G):
                     z_flipped = work.tile([P, C], F32, name="z_flipped")
-                    mean = mean_var[:, g * BN_AGGR : g * BN_AGGR + 1]
-                    nc.vector.tensor_scalar(z_flipped[:], x_flipped[b][:, g * C : (g + 1) * C], mean, rstd[:, g : g + 1], SUBTRACT, MULT)
+                    x_group = x_flipped[b][:, g * C : (g + 1) * C]
+                    if b < SCALAR_NORMALISES:
+                        nc.scalar.activation(z_flipped[:], x_group, FUNC.Identity, bias=shift[:, g : g + 1], scale=rstd[:, g : g + 1])
+                    else:
+                        mean = mean_var[:, g * BN_AGGR : g * BN_AGGR + 1]
+                        nc.vector.tensor_scalar(z_flipped[:], x_group, mean, rstd[:, g : g + 1], SUBTRACT, MULT)
                     for k in range(KB):
                         nc.tensor.transpose(back[k][:, g * P : (g + 1) * P], z_flipped[:, k * P : (k + 1) * P], identity[:])
                 for k in range(KB):

@@ -67,7 +67,7 @@ def tile_pclembeddings_kernel(tc, words, pos, tok, gamma, beta, offs, out):
 
         x_flipped = [held.tile([P, G * C], F32, name=f"x_flipped{b}") for b in range(B)]
 
-        with tc.psum_pool(name="psum_there", bufs=3) as psum_there, tc.psum_pool(name="psum_back", bufs=5) as psum_back:
+        with tc.psum_pool(name="psum_there", bufs=2) as psum_there, tc.psum_pool(name="psum_back", bufs=6) as psum_back:
 
             def look_up(k, b):
                 x = work.tile([P, T], F32, name="x")
@@ -96,7 +96,7 @@ def tile_pclembeddings_kernel(tc, words, pos, tok, gamma, beta, offs, out):
 
                 back = [psum_back.tile([P, T], F32, name="back") for k in range(KB)]
                 for g in range(G):
-                    z_flipped = work.tile([P, C], F32, name="z_flipped")
+                    z_flipped = work.tile([P, C], F32, name="z_flipped", bufs=8)
                     x_group = x_flipped[b][:, g * C : (g + 1) * C]
                     if b < SCALAR_NORMALISES:
                         nc.scalar.activation(z_flipped[:], x_group, FUNC.Identity, bias=shift[:, g : g + 1], scale=rstd[:, g : g + 1])
@@ -106,7 +106,7 @@ def tile_pclembeddings_kernel(tc, words, pos, tok, gamma, beta, offs, out):
                     for k in range(KB):
                         nc.tensor.transpose(back[k][:, g * P : (g + 1) * P], z_flipped[:, k * P : (k + 1) * P], identity[:])
                 for k in range(KB):
-                    y = work.tile([P, T], F32, name="y", bufs=8)
+                    y = work.tile([P, T], F32, name="y", bufs=12)
                     nc.scalar.activation(y[:], back[k][:], FUNC.Identity, bias=beta_col[k], scale=gamma_col[k])
                     nc.sync.dma_start(out_blocks[k][:, b * T : (b + 1) * T], y[:])
 

@@ -31,8 +31,6 @@ def tile_pclembeddings_kernel(tc, words, pos, tok, gamma, beta, offs, out):
     with tc.tile_pool(name="held", bufs=1) as held, tc.tile_pool(name="work", bufs=4) as work:
         eps = held.tile([P, 1], F32, name="eps")
         nc.vector.memset(eps[:], EPS)
-        table_warm_up = held.tile([P, 1], F32, name="table_warm_up")
-        nc.scalar.activation(table_warm_up[:], eps[:], FUNC.Abs_reciprocal_sqrt)
 
         offsets = held.tile([P, N // 16], U16, name="offsets")
         nc.sync.dma_start(offsets[:], offs)

import concourse.mybir as mybir
from concourse.masks import make_identity

F32 = mybir.dt.float32
U16 = mybir.dt.uint16
ADD = mybir.AluOpType.add
SUBTRACT = mybir.AluOpType.subtract
MULT = mybir.AluOpType.mult
FUNC = mybir.ActivationFunctionType

P = 128
C = 512
S = 4096
T = 512
B = 4
N = B * T
KB = C // P
G = T // P
EPS = 1e-5
SCALAR_NORMALISES = 1
BN_STATS = 6
BN_AGGR = 2


def tile_pclembeddings_kernel(tc, words, pos, tok, gamma, beta, offs, out):
    nc = tc.nc
    words_blocks = words.rearrange("(k p) s -> k p s", p=P)
    pos_blocks = pos.rearrange("(k p) t -> k p t", p=P)
    out_blocks = out.rearrange("(k p) n -> k p n", p=P)

    with tc.tile_pool(name="held", bufs=1) as held, tc.tile_pool(name="work", bufs=4) as work:
        eps = held.tile([P, 1], F32, name="eps")
        nc.vector.memset(eps[:], EPS)

        offsets = held.tile([P, N // 16], U16, name="offsets")
        nc.sync.dma_start(offsets[:], offs)

        postok = [held.tile([P, T], F32, name=f"postok{k}") for k in range(KB)]
        table = [held.tile([P, S], F32, name=f"table{k}") for k in range(KB)]
        nc.sync.dma_start(postok[0][:], pos_blocks[0])

        rows = held.tile([P, P], F32, name="rows")
        nc.gpsimd.memset(rows[:], 0.0)
        for i, vector in enumerate((tok, gamma, beta)):
            nc.sync.dma_start(rows[i * KB : (i + 1) * KB, :], vector.rearrange("(k p) o -> k (p o)", p=P))

        nc.sync.dma_start(table[0][:], words_blocks[0])
        for k in range(1, KB):
            nc.sync.dma_start(postok[k][:], pos_blocks[k])
            nc.sync.dma_start(table[k][:], words_blocks[k])

        identity = held.tile([P, P], F32, name="identity")
        make_identity(nc, identity[:])
        columns = held.tile([P, 3 * KB], F32, name="columns")
        with tc.psum_pool(name="psum_setup", bufs=1) as psum_setup:
            columns_psum = psum_setup.tile([P, P], F32, name="columns_psum")
            nc.tensor.transpose(columns_psum[:], rows[:], identity[:])
            nc.vector.tensor_copy(columns[:], columns_psum[:, 0 : 3 * KB])
        tok_col = [columns[:, 0 * KB + k : 0 * KB + k + 1] for k in range(KB)]
        gamma_col = [columns[:, 1 * KB + k : 1 * KB + k + 1] for k in range(KB)]
        beta_col = [columns[:, 2 * KB + k : 2 * KB + k + 1] for k in range(KB)]

        for k in range(KB):
            nc.scalar.activation(postok[k][:], postok[k][:], FUNC.Identity, bias=tok_col[k])

        x_flipped = [held.tile([P, G * C], F32, name=f"x_flipped{b}") for b in range(B)]

        with tc.psum_pool(name="psum_there", bufs=2) as psum_there, tc.psum_pool(name="psum_back", bufs=6) as psum_back:

            def look_up(k, b):
                x = work.tile([P, T], F32, name="x")
                nc.vector.tensor_tensor(x[:], table[k][:].indirect(offsets[:, b * T // 16 : (b + 1) * T // 16]), postok[k][:], ADD)
                there = psum_there.tile([P, G * P], F32, name="there")
                for g in range(G):
                    nc.tensor.transpose(there[:, g * P : (g + 1) * P], x[:, g * P : (g + 1) * P], identity[:])
                by_group = x_flipped[b][:].rearrange("t (g c) -> t g c", g=G)
                nc.scalar.activation(by_group[:, :, k * P : (k + 1) * P], there[:].rearrange("t (g c) -> t g c", g=G), FUNC.Identity)

            def normalise(b):
                stats = work.tile([P, G * BN_STATS], F32, name="stats")
                mean_var = work.tile([P, G * BN_AGGR], F32, name="mean_var")
                for g in range(G):
                    nc.vector.bn_stats(stats[:, g * BN_STATS : (g + 1) * BN_STATS], x_flipped[b][:, g * C : (g + 1) * C])
                    nc.vector.bn_aggr(mean_var[:, g * BN_AGGR : (g + 1) * BN_AGGR], stats[:, g * BN_STATS : (g + 1) * BN_STATS])
                if b < SCALAR_NORMALISES:
                    minus_mean = work.tile([P, G], F32, name="minus_mean")
                    nc.vector.tensor_scalar_mul(minus_mean[:], mean_var[:, 0 : G * BN_AGGR : BN_AGGR], -1.0)
                rstd = work.tile([P, G], F32, name="rstd")
                nc.scalar.activation(rstd[:], mean_var[:, 1 : G * BN_AGGR : BN_AGGR], FUNC.Abs_reciprocal_sqrt, bias=eps[:])
                if b < SCALAR_NORMALISES:
                    shift = work.tile([P, G], F32, name="shift")
                    for g in range(G):
                        nc.scalar.activation(shift[:, g : g + 1], minus_mean[:, g : g + 1], FUNC.Identity, scale=rstd[:, g : g + 1])

                back = [psum_back.tile([P, T], F32, name="back") for k in range(KB)]
                for g in range(G):
                    z_flipped = work.tile([P, C], F32, name="z_flipped", bufs=8)
                    x_group = x_flipped[b][:, g * C : (g + 1) * C]
                    if b < SCALAR_NORMALISES:
                        nc.scalar.activation(z_flipped[:], x_group, FUNC.Identity, bias=shift[:, g : g + 1], scale=rstd[:, g : g + 1])
                    else:
                        mean = mean_var[:, g * BN_AGGR : g * BN_AGGR + 1]
                        nc.vector.tensor_scalar(z_flipped[:], x_group, mean, rstd[:, g : g + 1], SUBTRACT, MULT)
                    for k in range(KB):
                        nc.tensor.transpose(back[k][:, g * P : (g + 1) * P], z_flipped[:, k * P : (k + 1) * P], identity[:])
                for k in range(KB):
                    y = work.tile([P, T], F32, name="y", bufs=12)
                    nc.scalar.activation(y[:], back[k][:], FUNC.Identity, bias=beta_col[k], scale=gamma_col[k])
                    nc.sync.dma_start(out_blocks[k][:, b * T : (b + 1) * T], y[:])

            for k in range(KB - 1):
                for b in range(B):
                    look_up(k, b)
            for b in range(B + 1):
                if b < B:
                    look_up(KB - 1, b)
                if b >= 1:
                    normalise(b - 1)
